import numpy as np
import ml_dtypes


def mxq(x, axis, fmt="e4m3"):
    dtype, down = {"e4m3": (ml_dtypes.float8_e4m3fn, 7), "e5m2": (ml_dtypes.float8_e5m2, 14)}[fmt]
    v = np.moveaxis(np.asarray(x, np.float32).astype(ml_dtypes.bfloat16).astype(np.float64), axis, -1)
    blocks = v.reshape(v.shape[:-1] + (-1, 32))
    amax = np.abs(blocks).max(-1, keepdims=True)
    byte = np.maximum(np.where(amax > 0, np.frexp(amax)[1] - 1 + 127, 0) - down, 1)
    scale = np.exp2(byte - 127.0)
    codes = (blocks / scale).astype(np.float32).astype(dtype).astype(np.float64)
    return np.moveaxis((codes * scale).reshape(v.shape), -1, axis)


WIDE = False


def mx_kscale(k):
    if not WIDE:
        return np.ones(k)
    levels = np.array([10, -10, 5, -5, 0])
    a = np.random.permutation(np.resize(levels, k // 512 * 4)).reshape(k // 512, 4)
    idx = np.arange(k)
    return np.exp2(a[idx // 512, idx % 128 // 32])


BF16 = ml_dtypes.bfloat16


def bf(x):
    return np.asarray(x, np.float32).astype(BF16)


def f64(x):
    return np.asarray(x).astype(np.float64)


B, T, KA, KT, DIM, NH, HD, E = 2, 512, 256, 256, 1024, 8, 128, 8
ROPE_BASE = 10000.0


def rope_cos_sin(L, hd):
    inv_freq = 1.0 / (ROPE_BASE ** (f64(np.arange(0, hd, 2)) / hd))
    freqs = f64(np.arange(L))[:, None] * inv_freq[None, :]
    emb = np.concatenate([freqs, freqs], axis=-1)
    return np.cos(emb), np.sin(emb)


def rotate_half(x):
    x1 = x[..., 0::2]
    x2 = x[..., 1::2]
    return np.stack((-x2, x1), axis=-1).reshape(x.shape)


def rope(t, cos, sin):
    return t * cos[None, None] + rotate_half(t) * sin[None, None]


def heads(t):
    return t.reshape(B, -1, NH, HD).transpose(0, 2, 1, 3)


def setup_inputs():
    s = mx_kscale(DIM)
    c = 1.2 / np.sqrt(DIM)
    return {"x": bf(np.random.standard_normal((B, T, DIM)) * s),
            "W_qa": bf(np.random.standard_normal((NH * HD, DIM)) * c / s[None, :]),
            "b_qa": bf(np.random.standard_normal(NH * HD) * 0.3),
            "W_qt": bf(np.random.standard_normal((NH * HD, DIM)) * c / s[None, :]),
            "b_qt": bf(np.random.standard_normal(NH * HD) * 0.3)}


def reference(x, W_qa, b_qa, W_qt, b_qt):
    xq = mxq(f64(x), 2, "e4m3")
    q_a = heads((xq @ mxq(f64(W_qa), 1, "e4m3").T) + f64(b_qa))
    q_t = heads((xq @ mxq(f64(W_qt), 1, "e4m3").T) + f64(b_qt))
    cos_m, sin_m = rope_cos_sin(T, HD)
    return rope(q_a, cos_m, sin_m), rope(q_t, cos_m, sin_m)

@@ -1,0 +1,261 @@
+import math
+from contextlib import ExitStack
+
+import concourse.bass as bass
+import concourse.mybir as mybir
+import concourse.tile as tile
+from concourse.masks import make_identity
+
+F32 = mybir.dt.float32
+BF16 = mybir.dt.bfloat16
+I32 = mybir.dt.int32
+U32 = mybir.dt.uint32
+U8 = mybir.dt.uint8
+FP8X4 = mybir.dt.float8_e4m3fn_x4
+ALU = mybir.AluOpType
+ACT = mybir.ActivationFunctionType
+
+P = 128
+FLOPS = 2 * 1024 * 1024 * 2048
+
+TWO_PI = 2.0 * math.pi
+C1 = 6.283203125
+C2 = TWO_PI - C1
+RATIO = 10000.0 ** (-1.0 / 64.0)
+
+
+def tile_l1regressionmoeactionhead_pa_kernel(tc, x, W_qa, b_qa, W_qt, b_qt, out_0, out_1):
+    nc = tc.nc
+    weights = [W_qa, W_qt]
+    outs = [out_0, out_1]
+    with ExitStack() as ctx:
+        keep = ctx.enter_context(tc.tile_pool(name="keep", bufs=1))
+        wgp = ctx.enter_context(tc.tile_pool(name="wgp", bufs=3))
+        qsp = ctx.enter_context(tc.tile_pool(name="qsp", bufs=2))
+        abp = ctx.enter_context(tc.tile_pool(name="abp", bufs=3))
+        obp = ctx.enter_context(tc.tile_pool(name="obp", bufs=4))
+        psum = ctx.enter_context(tc.psum_pool(name="psum", bufs=1))
+        ctx.enter_context(tc.manual_schedule())
+
+        def bank(tag):
+            return psum.tile([P, 512], F32, name="bk" + tag, tag=tag)
+
+        ident = keep.tile([P, P], F32, name="ident")
+        x_sb = [[keep.tile([P, 1024], BF16, name="x%d%d" % (n, j)) for j in range(4)] for n in range(2)]
+        w_sb = [keep.tile([P, 2048], BF16, name="w%d" % k) for k in range(8)]
+        xg = [keep.tile([P, 4096], BF16, name="xg%d" % n, align_bytes=64) for n in range(2)]
+        xcodes = [keep.tile([P, 1024], U32, name="xc%d" % n, align_bytes=64) for n in range(2)]
+        xscales = [keep.tile([P, 1024], U8, name="xs%d" % n, align_bytes=64) for n in range(2)]
+        wcodes = [keep.tile([P, 512], U32, name="wc%d" % k, align_bytes=64) for k in range(8)]
+        wscales = [keep.tile([P, 512], U8, name="ws%d" % k, align_bytes=64) for k in range(8)]
+        dm0 = keep.tile([P, 1], F32, name="dm0")
+        dm1 = keep.tile([P, 1], F32, name="dm1")
+        bz = keep.tile([P, 256], BF16, name="bz")
+        bf = keep.tile([P, 2, P], F32, name="bf")
+        bias_sb = keep.tile([P, 2, 8], F32, name="bias_sb")
+        freq = keep.tile([P, 64], F32, name="freq")
+        t_i = keep.tile([P, 4], I32, name="t_i")
+        t_f = keep.tile([P, 4], F32, name="t_f")
+        ang = keep.tile([P, 4, 64], F32, name="ang")
+        k_i = keep.tile([P, 4, 64], I32, name="k_i")
+        k_f = keep.tile([P, 4, 64], F32, name="k_f")
+        r1 = keep.tile([P, 4, 64], F32, name="r1")
+        r2 = keep.tile([P, 4, 64], F32, name="r2")
+        gs = keep.tile([P, 4, 64], F32, name="gs")
+        gc = keep.tile([P, 4, 64], F32, name="gc")
+        rs = keep.tile([P, 4, 64], F32, name="rs")
+        rc = keep.tile([P, 4, 64], F32, name="rc")
+        cos_t = keep.tile([P, 2, 4, 32], F32, name="cos_t")
+        sin_t = keep.tile([P, 2, 4, 32], F32, name="sin_t")
+
+        make_identity(nc, ident[:])
+        nc.gpsimd.iota(t_i[:], pattern=[[1, 4]], base=0, channel_multiplier=4)
+        nc.vector.memset(dm0[:], 0.0)
+        nc.vector.memset(bz[:], 0.0)
+        nc.vector.memset(freq[:, 0:1], 1.0)
+
+        nc.scalar.dma_start(out=bz[0:4, :], in_=b_qa.rearrange("(r c) -> r c", c=256))
+        nc.scalar.dma_start(out=bz[4:8, :], in_=b_qt.rearrange("(r c) -> r c", c=256))
+
+        def load_w(k):
+            rows = weights[k // 4][256 * (k % 4):256 * (k % 4) + 256, :]
+            nc.sync.dma_start(out=w_sb[k][:], in_=rows.rearrange("(p m) k -> p (m k)", m=2))
+
+        def load_x(n):
+            view = x[n].rearrange("(p j) k -> p j k", j=4)
+            for j in range(4):
+                nc.sync.dma_start(out=x_sb[n][j][:], in_=view[:, j, :])
+
+        load_w(0)
+        load_x(0)
+        for k in range(1, 8):
+            load_w(k)
+        load_x(1)
+
+        nc.scalar.activation(out=dm1[:], in_=dm0[:], func=ACT.Sin)
+
+        for c in range(1, 4):
+            nc.vector.tensor_scalar(out=freq[:, c:c + 1], in0=freq[:, 0:1], scalar1=RATIO ** c,
+                                    scalar2=None, op0=ALU.mult)
+        for a in range(1, 4):
+            nc.vector.tensor_scalar(out=freq[:, 4 * a:4 * a + 4], in0=freq[:, 0:4], scalar1=RATIO ** (4 * a),
+                                    scalar2=None, op0=ALU.mult)
+        for a in range(1, 4):
+            nc.vector.tensor_scalar(out=freq[:, 16 * a:16 * a + 16], in0=freq[:, 0:16], scalar1=RATIO ** (16 * a),
+                                    scalar2=None, op0=ALU.mult)
+        nc.vector.tensor_copy(out=t_f[:], in_=t_i[:])
+        nc.vector.tensor_tensor(out=ang[:], in0=freq[:].unsqueeze(1).to_broadcast([P, 4, 64]),
+                                in1=t_f[:].unsqueeze(2).to_broadcast([P, 4, 64]), op=ALU.mult)
+        nc.vector.tensor_scalar(out=k_i[:], in0=ang[:], scalar1=1.0 / TWO_PI, scalar2=None, op0=ALU.mult)
+        nc.vector.tensor_copy(out=k_f[:], in_=k_i[:])
+        nc.vector.tensor_copy(out=bf[:], in_=bz[:].rearrange("r (p m) -> r m p", m=2))
+        nc.vector.scalar_tensor_tensor(out=r1[:], in0=k_f[:], scalar=-C1, in1=ang[:], op0=ALU.mult, op1=ALU.add)
+        nc.vector.scalar_tensor_tensor(out=r2[:], in0=k_f[:], scalar=-C2, in1=r1[:], op0=ALU.mult, op1=ALU.add)
+        nc.vector.tensor_scalar(out=gs[:], in0=r2[:], scalar1=math.pi, scalar2=-TWO_PI, op0=ALU.is_gt, op1=ALU.mult)
+        nc.vector.tensor_scalar(out=gc[:], in0=r2[:], scalar1=0.5 * math.pi, scalar2=-TWO_PI,
+                                op0=ALU.is_gt, op1=ALU.mult)
+        nc.vector.tensor_tensor(out=rs[:], in0=r2[:], in1=gs[:], op=ALU.add)
+        nc.vector.scalar_tensor_tensor(out=rc[:], in0=r2[:], scalar=0.5 * math.pi, in1=gc[:],
+                                       op0=ALU.add, op1=ALU.add)
+
+        def words_in(src32, tag):
+            bk = bank(tag)
+            for q in range(4):
+                nc.tensor.transpose(bk[:, P * q:P * (q + 1)], src32[:, P * q:P * (q + 1)], ident[:])
+            return bk[:].rearrange("p (g u r) -> p g r u", g=2, u=2)
+
+        wg = {}
+
+        def w_in(k, m, tag):
+            if m == 0:
+                wg[k] = wgp.tile([P, 2048], BF16, name="wg", align_bytes=64)
+            src = words_in(w_sb[k][:].bitcast(F32)[:, 512 * m:512 * (m + 1)], tag)
+            dst = wg[k][:].bitcast(F32)[:, 512 * m:512 * (m + 1)].rearrange("p (g r u) -> p g r u", g=2, u=2)
+            nc.scalar.copy(out=dst, in_=src)
+
+        def w_quant(k):
+            nc.vector.quantize_mx(out=wcodes[k][:].bitcast(FP8X4), scales=wscales[k][:], in_=wg[k][:])
+
+        def x_in(n, j, tag, on_vector):
+            src = words_in(x_sb[n][j][:].bitcast(F32), tag)
+            dst = xg[n][:].bitcast(F32).rearrange("p (g c u) -> p g c u", g=2, u=2)[:, :, P * j:P * (j + 1), :]
+            if on_vector:
+                nc.vector.tensor_copy(out=dst, in_=src)
+            else:
+                nc.scalar.copy(out=dst, in_=src)
+
+        def x_quant(n, j):
+            for g in range(2):
+                c0 = 512 * g + P * j
+                nc.vector.quantize_mx(out=xcodes[n][:, c0:c0 + P].bitcast(FP8X4), scales=xscales[n][:, c0:c0 + P],
+                                      in_=xg[n][:, 4 * c0:4 * (c0 + P)])
+
+        acc = {}
+        qs = {}
+        tb = {}
+        ab = {}
+
+        def mx(i):
+            k, n = i % 8, i // 8
+            for m in range(2):
+                acc[(i, m)] = bank("ACC%d" % m)
+                for g in range(2):
+                    s0 = P * (2 * m + g)
+                    nc.tensor.matmul_mx(out=acc[(i, m)][:],
+                                        lhsT=wcodes[k][:, s0:s0 + P].bitcast(FP8X4),
+                                        lhsT_scale=wscales[k][:, s0:s0 + P],
+                                        rhs=xcodes[n][:, 512 * g:512 * (g + 1)].bitcast(FP8X4),
+                                        rhs_scale=xscales[n][:, 512 * g:512 * (g + 1)],
+                                        start=(g == 0), stop=(g == 1))
+
+        def add_bias(i):
+            k = i % 8
+            for m in range(2):
+                qs[(i, m)] = qsp.tile([P, 512], F32, name="qs%d" % m)
+                nc.scalar.activation(out=qs[(i, m)][:], in_=acc[(i, m)][:], func=ACT.Identity,
+                                     bias=bias_sb[:, m, k:k + 1], scale=1.0)
+
+        def back(i):
+            for m in range(2):
+                tb[(i, m)] = bank("T%d%d" % (i % 2, m))
+                for j in range(4):
+                    nc.tensor.transpose(tb[(i, m)][:, P * j:P * (j + 1)], qs[(i, m)][:, P * j:P * (j + 1)], ident[:])
+
+        def rope(i, m):
+            if m == 0:
+                ab[i] = abp.tile([P, 2, 2, 512], F32, name="ab")
+            tv = tb[(i, m)][:].rearrange("p (j r c) -> p j r c", j=4, r=4)
+            nc.vector.tensor_tensor(out=ab[i][:, 0, m, :].rearrange("p (j r c) -> p j r c", j=4, r=4), in0=tv,
+                                    in1=cos_t[:, m, :, :].unsqueeze(2).to_broadcast([P, 4, 4, 32]), op=ALU.mult)
+            nc.vector.tensor_tensor(out=ab[i][:, 1, 1 - m, :].rearrange("p (j r c) -> p j r c", j=4, r=4), in0=tv,
+                                    in1=sin_t[:, 1 - m, :, :].unsqueeze(2).to_broadcast([P, 4, 4, 32]), op=ALU.mult)
+
+        def add_store(i):
+            k, n = i % 8, i // 8
+            ob = obp.tile([P, 2, 512], F32, name="ob")
+            for h in range(2):
+                a_v = ab[i][:, 0, :, :].rearrange("p e (j h c) -> p h j c e", j=4, h=2)[:, h]
+                b_v = ab[i][:, 1, :, :].rearrange("p e (j h c) -> p h j c e", j=4, h=2)[:, h]
+                nc.gpsimd.tensor_tensor(out=ob[:, h, :].rearrange("p (j c e) -> p j c e", j=4, e=2),
+                                        in0=a_v, in1=b_v, op=ALU.add)
+            head = 2 * (k % 4)
+            nc.sync.dma_start(out=outs[k // 4][n, head:head + 2].rearrange("h (p j) d -> p h (j d)", j=4), in_=ob[:])
+
+        w_in(0, 0, "IN0")
+        w_in(0, 1, "IN1")
+        x_in(0, 0, "T00", True)
+        x_in(0, 1, "T01", False)
+        w_quant(0)
+        x_quant(0, 0)
+        x_in(0, 2, "T10", True)
+        x_quant(0, 1)
+        nc.scalar.activation(out=cos_t[:], in_=rc[:].rearrange("p j (c e) -> p e j c", e=2), func=ACT.Sin)
+        rs_v = rs[:].rearrange("p j (c e) -> p e j c", e=2)
+        nc.scalar.activation(out=sin_t[:, 0], in_=rs_v[:, 0], func=ACT.Sin, scale=-1.0)
+        nc.scalar.activation(out=sin_t[:, 1], in_=rs_v[:, 1], func=ACT.Sin)
+        x_in(0, 3, "T11", False)
+        x_quant(0, 2)
+        x_quant(0, 3)
+        bias_ps = bank("ACC1")
+        for m in range(2):
+            nc.tensor.transpose(bias_ps[:, P * m:P * (m + 1)], bf[:, m, :], ident[:])
+        nc.scalar.copy(out=bias_sb[:], in_=bias_ps[:, 0:256].rearrange("p (m r) -> p m r", m=2)[:, :, 0:8])
+        w_in(1, 0, "IN0")
+        w_in(1, 1, "IN1")
+        w_quant(1)
+
+        for i in range(8):
+            mx(i)
+            add_bias(i)
+            if i < 6:
+                w_in(i + 2, 0, "IN0")
+                w_in(i + 2, 1, "IN1")
+            else:
+                x_in(1, 2 * (i - 6), "IN0", False)
+                x_in(1, 2 * (i - 6) + 1, "IN1", False)
+            back(i)
+            if i == 7:
+                x_quant(1, 2)
+                x_quant(1, 3)
+            rope(i, 0)
+            if i < 6:
+                w_quant(i + 2)
+            elif i == 6:
+                x_quant(1, 0)
+                x_quant(1, 1)
+            rope(i, 1)
+            add_store(i)
+
+        mx(8)
+        add_bias(8)
+        for i in range(9, 16):
+            mx(i)
+            add_bias(i)
+            back(i - 1)
+            rope(i - 1, 0)
+            rope(i - 1, 1)
+            add_store(i - 1)
+        back(15)
+        rope(15, 0)
+        rope(15, 1)
+        add_store(15)

@@ -32,7 +32,7 @@ def tile_l1regressionmoeactionhead_pa_kernel(tc, x, W_qa, b_qa, W_qt, b_qt, out_
         keep = ctx.enter_context(tc.tile_pool(name="keep", bufs=1))
         wgp = ctx.enter_context(tc.tile_pool(name="wgp", bufs=3))
         qsp = ctx.enter_context(tc.tile_pool(name="qsp", bufs=2))
-        abp = ctx.enter_context(tc.tile_pool(name="abp", bufs=3))
+        abp = ctx.enter_context(tc.tile_pool(name="abp", bufs=4))
         obp = ctx.enter_context(tc.tile_pool(name="obp", bufs=4))
         psum = ctx.enter_context(tc.psum_pool(name="psum", bufs=1))
         ctx.enter_context(tc.manual_schedule())
@@ -190,16 +190,32 @@ def tile_l1regressionmoeactionhead_pa_kernel(tc, x, W_qa, b_qa, W_qt, b_qt, out_
             nc.vector.tensor_tensor(out=ab[i][:, 1, 1 - m, :].rearrange("p (j r c) -> p j r c", j=4, r=4), in0=tv,
                                     in1=sin_t[:, 1 - m, :, :].unsqueeze(2).to_broadcast([P, 4, 4, 32]), op=ALU.mult)
 
-        def add_store(i):
+        ob = {}
+        on_vector_adds = [1, 3, 5, 7, 9, 10, 11, 13, 14, 15]
+
+        def add(i, h, eng):
+            a_v = ab[i][:, 0, :, :].rearrange("p e (j h c) -> p h j c e", j=4, h=2)[:, h]
+            b_v = ab[i][:, 1, :, :].rearrange("p e (j h c) -> p h j c e", j=4, h=2)[:, h]
+            eng.tensor_tensor(out=ob[i][:, h, :].rearrange("p (j c e) -> p j c e", j=4, e=2),
+                              in0=a_v, in1=b_v, op=ALU.add)
+
+        def adds_gpsimd(i):
+            ob[i] = obp.tile([P, 2, 512], F32, name="ob")
+            add(i, 0, nc.gpsimd)
+            if i not in on_vector_adds:
+                add(i, 1, nc.gpsimd)
+
+        def add_vector(i):
+            if i >= 0 and i in on_vector_adds:
+                add(i, 1, nc.vector)
+
+        def store(i):
+            if i < 0:
+                return
             k, n = i % 8, i // 8
-            ob = obp.tile([P, 2, 512], F32, name="ob")
-            for h in range(2):
-                a_v = ab[i][:, 0, :, :].rearrange("p e (j h c) -> p h j c e", j=4, h=2)[:, h]
-                b_v = ab[i][:, 1, :, :].rearrange("p e (j h c) -> p h j c e", j=4, h=2)[:, h]
-                nc.gpsimd.tensor_tensor(out=ob[:, h, :].rearrange("p (j c e) -> p j c e", j=4, e=2),
-                                        in0=a_v, in1=b_v, op=ALU.add)
             head = 2 * (k % 4)
-            nc.sync.dma_start(out=outs[k // 4][n, head:head + 2].rearrange("h (p j) d -> p h (j d)", j=4), in_=ob[:])
+            nc.sync.dma_start(out=outs[k // 4][n, head:head + 2].rearrange("h (p j) d -> p h (j d)", j=4),
+                              in_=ob[i][:])
 
         w_in(0, 0, "IN0")
         w_in(0, 1, "IN1")
@@ -238,13 +254,15 @@ def tile_l1regressionmoeactionhead_pa_kernel(tc, x, W_qa, b_qa, W_qt, b_qt, out_
                 x_quant(1, 2)
                 x_quant(1, 3)
             rope(i, 0)
+            add_vector(i - 1)
+            store(i - 1)
             if i < 6:
                 w_quant(i + 2)
             elif i == 6:
                 x_quant(1, 0)
                 x_quant(1, 1)
             rope(i, 1)
-            add_store(i)
+            adds_gpsimd(i)
 
         mx(8)
         add_bias(8)
@@ -253,9 +271,15 @@ def tile_l1regressionmoeactionhead_pa_kernel(tc, x, W_qa, b_qa, W_qt, b_qt, out_
             add_bias(i)
             back(i - 1)
             rope(i - 1, 0)
+            add_vector(i - 2)
+            store(i - 2)
             rope(i - 1, 1)
-            add_store(i - 1)
+            adds_gpsimd(i - 1)
         back(15)
         rope(15, 0)
+        add_vector(14)
+        store(14)
         rope(15, 1)
-        add_store(15)
+        adds_gpsimd(15)
+        add_vector(15)
+        store(15)

@@ -31,7 +31,7 @@ def tile_l1regressionmoeactionhead_pa_kernel(tc, x, W_qa, b_qa, W_qt, b_qt, out_
     with ExitStack() as ctx:
         keep = ctx.enter_context(tc.tile_pool(name="keep", bufs=1))
         wgp = ctx.enter_context(tc.tile_pool(name="wgp", bufs=3))
-        qsp = ctx.enter_context(tc.tile_pool(name="qsp", bufs=2))
+        qsp = ctx.enter_context(tc.tile_pool(name="qsp", bufs=3))
         abp = ctx.enter_context(tc.tile_pool(name="abp", bufs=4))
         obp = ctx.enter_context(tc.tile_pool(name="obp", bufs=4))
         psum = ctx.enter_context(tc.psum_pool(name="psum", bufs=1))
@@ -88,9 +88,10 @@ def tile_l1regressionmoeactionhead_pa_kernel(tc, x, W_qa, b_qa, W_qt, b_qt, out_
 
         load_w(0)
         load_x(0)
-        for k in range(1, 8):
-            load_w(k)
+        load_w(1)
         load_x(1)
+        for k in range(2, 8):
+            load_w(k)
 
         nc.scalar.activation(out=dm1[:], in_=dm0[:], func=ACT.Sin)
 
@@ -111,12 +112,6 @@ def tile_l1regressionmoeactionhead_pa_kernel(tc, x, W_qa, b_qa, W_qt, b_qt, out_
         nc.vector.tensor_copy(out=bf[:], in_=bz[:].rearrange("r (p m) -> r m p", m=2))
         nc.vector.scalar_tensor_tensor(out=r1[:], in0=k_f[:], scalar=-C1, in1=ang[:], op0=ALU.mult, op1=ALU.add)
         nc.vector.scalar_tensor_tensor(out=r2[:], in0=k_f[:], scalar=-C2, in1=r1[:], op0=ALU.mult, op1=ALU.add)
-        nc.vector.tensor_scalar(out=gs[:], in0=r2[:], scalar1=math.pi, scalar2=-TWO_PI, op0=ALU.is_gt, op1=ALU.mult)
-        nc.vector.tensor_scalar(out=gc[:], in0=r2[:], scalar1=0.5 * math.pi, scalar2=-TWO_PI,
-                                op0=ALU.is_gt, op1=ALU.mult)
-        nc.vector.tensor_tensor(out=rs[:], in0=r2[:], in1=gs[:], op=ALU.add)
-        nc.vector.scalar_tensor_tensor(out=rc[:], in0=r2[:], scalar=0.5 * math.pi, in1=gc[:],
-                                       op0=ALU.add, op1=ALU.add)
 
         def words_in(src32, tag):
             bk = bank(tag)
@@ -150,13 +145,14 @@ def tile_l1regressionmoeactionhead_pa_kernel(tc, x, W_qa, b_qa, W_qt, b_qt, out_
                 nc.vector.quantize_mx(out=xcodes[n][:, c0:c0 + P].bitcast(FP8X4), scales=xscales[n][:, c0:c0 + P],
                                       in_=xg[n][:, 4 * c0:4 * (c0 + P)])
 
+        rounds = [(0, 0), (1, 0), (0, 1), (1, 1)] + [(k, n) for k in range(2, 8) for n in range(2)]
         acc = {}
         qs = {}
         tb = {}
         ab = {}
 
         def mx(i):
-            k, n = i % 8, i // 8
+            k, n = rounds[i]
             for m in range(2):
                 acc[(i, m)] = bank("ACC%d" % m)
                 for g in range(2):
@@ -169,7 +165,7 @@ def tile_l1regressionmoeactionhead_pa_kernel(tc, x, W_qa, b_qa, W_qt, b_qt, out_
                                         start=(g == 0), stop=(g == 1))
 
         def add_bias(i):
-            k = i % 8
+            k = rounds[i][0]
             for m in range(2):
                 qs[(i, m)] = qsp.tile([P, 512], F32, name="qs%d" % m)
                 nc.scalar.activation(out=qs[(i, m)][:], in_=acc[(i, m)][:], func=ACT.Identity,
@@ -191,7 +187,7 @@ def tile_l1regressionmoeactionhead_pa_kernel(tc, x, W_qa, b_qa, W_qt, b_qt, out_
                                     in1=sin_t[:, 1 - m, :, :].unsqueeze(2).to_broadcast([P, 4, 4, 32]), op=ALU.mult)
 
         ob = {}
-        on_vector_adds = [1, 3, 5, 7, 9, 10, 11, 13, 14, 15]
+        on_vector_adds = [3, 6, 9, 11, 13, 14, 15]
 
         def add(i, h, eng):
             a_v = ab[i][:, 0, :, :].rearrange("p e (j h c) -> p h j c e", j=4, h=2)[:, h]
@@ -212,26 +208,26 @@ def tile_l1regressionmoeactionhead_pa_kernel(tc, x, W_qa, b_qa, W_qt, b_qt, out_
         def store(i):
             if i < 0:
                 return
-            k, n = i % 8, i // 8
+            k, n = rounds[i]
             head = 2 * (k % 4)
             nc.sync.dma_start(out=outs[k // 4][n, head:head + 2].rearrange("h (p j) d -> p h (j d)", j=4),
                               in_=ob[i][:])
 
         w_in(0, 0, "IN0")
         w_in(0, 1, "IN1")
-        x_in(0, 0, "T00", True)
-        x_in(0, 1, "T01", False)
-        w_quant(0)
-        x_quant(0, 0)
-        x_in(0, 2, "T10", True)
-        x_quant(0, 1)
-        nc.scalar.activation(out=cos_t[:], in_=rc[:].rearrange("p j (c e) -> p e j c", e=2), func=ACT.Sin)
-        rs_v = rs[:].rearrange("p j (c e) -> p e j c", e=2)
-        nc.scalar.activation(out=sin_t[:, 0], in_=rs_v[:, 0], func=ACT.Sin, scale=-1.0)
-        nc.scalar.activation(out=sin_t[:, 1], in_=rs_v[:, 1], func=ACT.Sin)
-        x_in(0, 3, "T11", False)
-        x_quant(0, 2)
+        for j in range(4):
+            x_in(0, j, "T%d%d" % (j // 2, j % 2), False)
+            if j == 0:
+                w_quant(0)
+            else:
+                x_quant(0, j - 1)
         x_quant(0, 3)
+        nc.vector.tensor_scalar(out=gs[:], in0=r2[:], scalar1=math.pi, scalar2=-TWO_PI, op0=ALU.is_gt, op1=ALU.mult)
+        nc.vector.tensor_scalar(out=gc[:], in0=r2[:], scalar1=0.5 * math.pi, scalar2=-TWO_PI,
+                                op0=ALU.is_gt, op1=ALU.mult)
+        nc.vector.tensor_tensor(out=rs[:], in0=r2[:], in1=gs[:], op=ALU.add)
+        nc.vector.scalar_tensor_tensor(out=rc[:], in0=r2[:], scalar=0.5 * math.pi, in1=gc[:],
+                                       op0=ALU.add, op1=ALU.add)
         bias_ps = bank("ACC1")
         for m in range(2):
             nc.tensor.transpose(bias_ps[:, P * m:P * (m + 1)], bf[:, m, :], ident[:])
@@ -239,42 +235,44 @@ def tile_l1regressionmoeactionhead_pa_kernel(tc, x, W_qa, b_qa, W_qt, b_qt, out_
         w_in(1, 0, "IN0")
         w_in(1, 1, "IN1")
         w_quant(1)
+        mx(0)
+        nc.scalar.activation(out=cos_t[:], in_=rc[:].rearrange("p j (c e) -> p e j c", e=2), func=ACT.Sin)
+        rs_v = rs[:].rearrange("p j (c e) -> p e j c", e=2)
+        nc.scalar.activation(out=sin_t[:, 0], in_=rs_v[:, 0], func=ACT.Sin, scale=-1.0)
+        nc.scalar.activation(out=sin_t[:, 1], in_=rs_v[:, 1], func=ACT.Sin)
+        add_bias(0)
+        x_in(1, 0, "T10", False)
+        x_in(1, 1, "T11", False)
+        x_in(1, 2, "IN0", False)
+        x_in(1, 3, "IN1", False)
+        back(0)
+        x_quant(1, 0)
+        x_quant(1, 1)
 
-        for i in range(8):
-            mx(i)
-            add_bias(i)
-            if i < 6:
-                w_in(i + 2, 0, "IN0")
-                w_in(i + 2, 1, "IN1")
-            else:
-                x_in(1, 2 * (i - 6), "IN0", False)
-                x_in(1, 2 * (i - 6) + 1, "IN1", False)
-            back(i)
-            if i == 7:
+        jobs = {}
+        for k in range(2, 8):
+            for m in range(2):
+                r = max(1, 2 * k - 4 + m)
+                jobs[r] = jobs.get(r, []) + [(k, m)]
+        n_jobs = 0
+        for r in range(1, 16):
+            mx(r)
+            add_bias(r)
+            if r > 1:
+                back(r - 1)
+            for (k, m) in jobs.get(r, []):
+                w_in(k, m, "IN%d" % (n_jobs % 2))
+                n_jobs += 1
+            rope(r - 1, 0)
+            if r == 1:
                 x_quant(1, 2)
                 x_quant(1, 3)
-            rope(i, 0)
-            add_vector(i - 1)
-            store(i - 1)
-            if i < 6:
-                w_quant(i + 2)
-            elif i == 6:
-                x_quant(1, 0)
-                x_quant(1, 1)
-            rope(i, 1)
-            adds_gpsimd(i)
-
-        mx(8)
-        add_bias(8)
-        for i in range(9, 16):
-            mx(i)
-            add_bias(i)
-            back(i - 1)
-            rope(i - 1, 0)
-            add_vector(i - 2)
-            store(i - 2)
-            rope(i - 1, 1)
-            adds_gpsimd(i - 1)
+            add_vector(r - 2)
+            store(r - 2)
+            if r % 2 == 0 and 2 <= r <= 12:
+                w_quant(r // 2 + 1)
+            rope(r - 1, 1)
+            adds_gpsimd(r - 1)
         back(15)
         rope(15, 0)
         add_vector(14)

@@ -151,9 +151,9 @@ def tile_l1regressionmoeactionhead_pa_kernel(tc, x, W_qa, b_qa, W_qt, b_qt, out_
         tb = {}
         ab = {}
 
-        def mx(i):
+        def mx(i, tiles=(0, 1)):
             k, n = rounds[i]
-            for m in range(2):
+            for m in tiles:
                 acc[(i, m)] = bank("ACC%d" % m)
                 for g in range(2):
                     s0 = P * (2 * m + g)
@@ -164,15 +164,15 @@ def tile_l1regressionmoeactionhead_pa_kernel(tc, x, W_qa, b_qa, W_qt, b_qt, out_
                                         rhs_scale=xscales[n][:, 512 * g:512 * (g + 1)],
                                         start=(g == 0), stop=(g == 1))
 
-        def add_bias(i):
+        def add_bias(i, tiles=(0, 1)):
             k = rounds[i][0]
-            for m in range(2):
+            for m in tiles:
                 qs[(i, m)] = qsp.tile([P, 512], F32, name="qs%d" % m)
                 nc.scalar.activation(out=qs[(i, m)][:], in_=acc[(i, m)][:], func=ACT.Identity,
                                      bias=bias_sb[:, m, k:k + 1], scale=1.0)
 
-        def back(i):
-            for m in range(2):
+        def back(i, tiles=(0, 1)):
+            for m in tiles:
                 tb[(i, m)] = bank("T%d%d" % (i % 2, m))
                 for j in range(4):
                     nc.tensor.transpose(tb[(i, m)][:, P * j:P * (j + 1)], qs[(i, m)][:, P * j:P * (j + 1)], ident[:])
@@ -256,10 +256,11 @@ def tile_l1regressionmoeactionhead_pa_kernel(tc, x, W_qa, b_qa, W_qt, b_qt, out_
                 jobs[r] = jobs.get(r, []) + [(k, m)]
         n_jobs = 0
         for r in range(1, 16):
-            mx(r)
-            add_bias(r)
-            if r > 1:
-                back(r - 1)
+            for m in range(2):
+                mx(r, (m,))
+                add_bias(r, (m,))
+                if r > 1:
+                    back(r - 1, (m,))
             for (k, m) in jobs.get(r, []):
                 w_in(k, m, "IN%d" % (n_jobs % 2))
                 n_jobs += 1

@@ -1,9 +1,7 @@
 import math
 from contextlib import ExitStack
 
-import concourse.bass as bass
 import concourse.mybir as mybir
-import concourse.tile as tile
 from concourse.masks import make_identity
 
 F32 = mybir.dt.float32
@@ -22,6 +20,9 @@ TWO_PI = 2.0 * math.pi
 C1 = 6.283203125
 C2 = TWO_PI - C1
 RATIO = 10000.0 ** (-1.0 / 64.0)
+N_ROUNDS = 16
+LAST_DIRECT = 6
+FIRST_VECTOR_ADD = 14
 
 
 def tile_l1regressionmoeactionhead_pa_kernel(tc, x, W_qa, b_qa, W_qt, b_qt, out_0, out_1):
@@ -32,7 +33,7 @@ def tile_l1regressionmoeactionhead_pa_kernel(tc, x, W_qa, b_qa, W_qt, b_qt, out_
         keep = ctx.enter_context(tc.tile_pool(name="keep", bufs=1))
         wgp = ctx.enter_context(tc.tile_pool(name="wgp", bufs=3))
         qsp = ctx.enter_context(tc.tile_pool(name="qsp", bufs=3))
-        abp = ctx.enter_context(tc.tile_pool(name="abp", bufs=4))
+        abp = ctx.enter_context(tc.tile_pool(name="abp", bufs=5))
         obp = ctx.enter_context(tc.tile_pool(name="obp", bufs=4))
         psum = ctx.enter_context(tc.psum_pool(name="psum", bufs=1))
         ctx.enter_context(tc.manual_schedule())
@@ -65,8 +66,8 @@ def tile_l1regressionmoeactionhead_pa_kernel(tc, x, W_qa, b_qa, W_qt, b_qt, out_
         gc = keep.tile([P, 4, 64], F32, name="gc")
         rs = keep.tile([P, 4, 64], F32, name="rs")
         rc = keep.tile([P, 4, 64], F32, name="rc")
-        cos_t = keep.tile([P, 2, 4, 32], F32, name="cos_t")
-        sin_t = keep.tile([P, 2, 4, 32], F32, name="sin_t")
+        cos_t = keep.tile([P, 2, 4, 2, 32], F32, name="cos_t")
+        sin_t = keep.tile([P, 2, 4, 2, 32], F32, name="sin_t")
 
         make_identity(nc, ident[:])
         nc.gpsimd.iota(t_i[:], pattern=[[1, 4]], base=0, channel_multiplier=4)
@@ -131,13 +132,10 @@ def tile_l1regressionmoeactionhead_pa_kernel(tc, x, W_qa, b_qa, W_qt, b_qt, out_
         def w_quant(k):
             nc.vector.quantize_mx(out=wcodes[k][:].bitcast(FP8X4), scales=wscales[k][:], in_=wg[k][:])
 
-        def x_in(n, j, tag, on_vector):
+        def x_in(n, j, tag):
             src = words_in(x_sb[n][j][:].bitcast(F32), tag)
             dst = xg[n][:].bitcast(F32).rearrange("p (g c u) -> p g c u", g=2, u=2)[:, :, P * j:P * (j + 1), :]
-            if on_vector:
-                nc.vector.tensor_copy(out=dst, in_=src)
-            else:
-                nc.scalar.copy(out=dst, in_=src)
+            nc.scalar.copy(out=dst, in_=src)
 
         def x_quant(n, j):
             for g in range(2):
@@ -151,9 +149,9 @@ def tile_l1regressionmoeactionhead_pa_kernel(tc, x, W_qa, b_qa, W_qt, b_qt, out_
         tb = {}
         ab = {}
 
-        def mx(i, tiles=(0, 1)):
+        def mx(i):
             k, n = rounds[i]
-            for m in tiles:
+            for m in range(2):
                 acc[(i, m)] = bank("ACC%d" % m)
                 for g in range(2):
                     s0 = P * (2 * m + g)
@@ -163,60 +161,53 @@ def tile_l1regressionmoeactionhead_pa_kernel(tc, x, W_qa, b_qa, W_qt, b_qt, out_
                                         rhs=xcodes[n][:, 512 * g:512 * (g + 1)].bitcast(FP8X4),
                                         rhs_scale=xscales[n][:, 512 * g:512 * (g + 1)],
                                         start=(g == 0), stop=(g == 1))
-
-        def add_bias(i, tiles=(0, 1)):
-            k = rounds[i][0]
-            for m in tiles:
+            for m in range(2):
                 qs[(i, m)] = qsp.tile([P, 512], F32, name="qs%d" % m)
                 nc.scalar.activation(out=qs[(i, m)][:], in_=acc[(i, m)][:], func=ACT.Identity,
                                      bias=bias_sb[:, m, k:k + 1], scale=1.0)
 
-        def back(i, tiles=(0, 1)):
-            for m in tiles:
+        ident_hc = ident[:].rearrange("p (h c) -> p h c", h=2)
+
+        def back(i):
+            for m in range(2):
                 tb[(i, m)] = bank("T%d%d" % (i % 2, m))
+                by_head = tb[(i, m)][:].rearrange("p (h j c) -> p h j c", h=2, j=4)
                 for j in range(4):
-                    nc.tensor.transpose(tb[(i, m)][:, P * j:P * (j + 1)], qs[(i, m)][:, P * j:P * (j + 1)], ident[:])
+                    nc.tensor.transpose(by_head[:, :, j, :], qs[(i, m)][:, P * j:P * (j + 1)], ident_hc)
 
-        def rope(i, m):
-            if m == 0:
+        def rope(i, tiles=(0, 1)):
+            if 0 in tiles:
                 ab[i] = abp.tile([P, 2, 2, 512], F32, name="ab")
-            tv = tb[(i, m)][:].rearrange("p (j r c) -> p j r c", j=4, r=4)
-            nc.vector.tensor_tensor(out=ab[i][:, 0, m, :].rearrange("p (j r c) -> p j r c", j=4, r=4), in0=tv,
-                                    in1=cos_t[:, m, :, :].unsqueeze(2).to_broadcast([P, 4, 4, 32]), op=ALU.mult)
-            nc.vector.tensor_tensor(out=ab[i][:, 1, 1 - m, :].rearrange("p (j r c) -> p j r c", j=4, r=4), in0=tv,
-                                    in1=sin_t[:, 1 - m, :, :].unsqueeze(2).to_broadcast([P, 4, 4, 32]), op=ALU.mult)
+            for m in tiles:
+                tv = tb[(i, m)][:].rearrange("p (h c) -> p h c", h=2)
+                cos_v = cos_t[:, m].rearrange("p j r c -> p (j r c)").unsqueeze(1).to_broadcast([P, 2, 256])
+                sin_v = sin_t[:, 1 - m].rearrange("p j r c -> p (j r c)").unsqueeze(1).to_broadcast([P, 2, 256])
+                nc.vector.tensor_tensor(out=ab[i][:, 0, m, :].rearrange("p (h c) -> p h c", h=2), in0=tv,
+                                        in1=cos_v, op=ALU.mult)
+                nc.vector.tensor_tensor(out=ab[i][:, 1, 1 - m, :].rearrange("p (h c) -> p h c", h=2), in0=tv,
+                                        in1=sin_v, op=ALU.mult)
 
-        ob = {}
-        on_vector_adds = [3, 6, 9, 11, 13, 14, 15]
-
-        def add(i, h, eng):
-            a_v = ab[i][:, 0, :, :].rearrange("p e (j h c) -> p h j c e", j=4, h=2)[:, h]
-            b_v = ab[i][:, 1, :, :].rearrange("p e (j h c) -> p h j c e", j=4, h=2)[:, h]
-            eng.tensor_tensor(out=ob[i][:, h, :].rearrange("p (j c e) -> p j c e", j=4, e=2),
-                              in0=a_v, in1=b_v, op=ALU.add)
-
-        def adds_gpsimd(i):
-            ob[i] = obp.tile([P, 2, 512], F32, name="ob")
-            add(i, 0, nc.gpsimd)
-            if i not in on_vector_adds:
-                add(i, 1, nc.gpsimd)
-
-        def add_vector(i):
-            if i >= 0 and i in on_vector_adds:
-                add(i, 1, nc.vector)
-
-        def store(i):
-            if i < 0:
-                return
+        def add_store(i):
             k, n = rounds[i]
             head = 2 * (k % 4)
-            nc.sync.dma_start(out=outs[k // 4][n, head:head + 2].rearrange("h (p j) d -> p h (j d)", j=4),
-                              in_=ob[i][:])
+            dst = outs[k // 4][n, head:head + 2].rearrange("h (p j) d -> p h (j d)", j=4)
+            ob = obp.tile([P, 2, 512], F32, name="ob")
+            a_v = ab[i][:, 0].rearrange("p e c -> p c e")
+            b_v = ab[i][:, 1].rearrange("p e c -> p c e")
+            o_v = ob[:].rearrange("p h (c e) -> p (h c) e", e=2)
+            if i < FIRST_VECTOR_ADD:
+                nc.gpsimd.tensor_tensor(out=o_v, in0=a_v, in1=b_v, op=ALU.add)
+                nc.sync.dma_start(out=dst, in_=ob[:])
+            else:
+                for h in range(2):
+                    cols = slice(256 * h, 256 * (h + 1))
+                    nc.vector.tensor_tensor(out=o_v[:, cols, :], in0=a_v[:, cols, :], in1=b_v[:, cols, :], op=ALU.add)
+                    nc.sync.dma_start(out=dst[:, h, :], in_=ob[:, h, :])
 
         w_in(0, 0, "IN0")
         w_in(0, 1, "IN1")
         for j in range(4):
-            x_in(0, j, "T%d%d" % (j // 2, j % 2), False)
+            x_in(0, j, "T%d%d" % (j // 2, j % 2))
             if j == 0:
                 w_quant(0)
             else:
@@ -235,50 +226,39 @@ def tile_l1regressionmoeactionhead_pa_kernel(tc, x, W_qa, b_qa, W_qt, b_qt, out_
         w_in(1, 0, "IN0")
         w_in(1, 1, "IN1")
         w_quant(1)
+        for e in range(2):
+            rc_v = rc[:].rearrange("p j (c e) -> p e j c", e=2)[:, e].unsqueeze(2).to_broadcast([P, 4, 2, 32])
+            rs_v = rs[:].rearrange("p j (c e) -> p e j c", e=2)[:, e].unsqueeze(2).to_broadcast([P, 4, 2, 32])
+            nc.scalar.activation(out=cos_t[:, e], in_=rc_v, func=ACT.Sin)
+            nc.scalar.activation(out=sin_t[:, e], in_=rs_v, func=ACT.Sin, scale=(-1.0 if e == 0 else 1.0))
         mx(0)
-        nc.scalar.activation(out=cos_t[:], in_=rc[:].rearrange("p j (c e) -> p e j c", e=2), func=ACT.Sin)
-        rs_v = rs[:].rearrange("p j (c e) -> p e j c", e=2)
-        nc.scalar.activation(out=sin_t[:, 0], in_=rs_v[:, 0], func=ACT.Sin, scale=-1.0)
-        nc.scalar.activation(out=sin_t[:, 1], in_=rs_v[:, 1], func=ACT.Sin)
-        add_bias(0)
-        x_in(1, 0, "T10", False)
-        x_in(1, 1, "T11", False)
-        x_in(1, 2, "IN0", False)
-        x_in(1, 3, "IN1", False)
+        x_in(1, 0, "T10")
+        x_in(1, 1, "T11")
+        x_in(1, 2, "IN0")
+        x_in(1, 3, "IN1")
         back(0)
         x_quant(1, 0)
         x_quant(1, 1)
+        rope(0, (0,))
+        x_quant(1, 2)
+        x_quant(1, 3)
+        rope(0, (1,))
+        add_store(0)
 
-        jobs = {}
-        for k in range(2, 8):
-            for m in range(2):
-                r = max(1, 2 * k - 4 + m)
-                jobs[r] = jobs.get(r, []) + [(k, m)]
-        n_jobs = 0
-        for r in range(1, 16):
-            for m in range(2):
-                mx(r, (m,))
-                add_bias(r, (m,))
-                if r > 1:
-                    back(r - 1, (m,))
-            for (k, m) in jobs.get(r, []):
-                w_in(k, m, "IN%d" % (n_jobs % 2))
-                n_jobs += 1
-            rope(r - 1, 0)
-            if r == 1:
-                x_quant(1, 2)
-                x_quant(1, 3)
-            add_vector(r - 2)
-            store(r - 2)
-            if r % 2 == 0 and 2 <= r <= 12:
-                w_quant(r // 2 + 1)
-            rope(r - 1, 1)
-            adds_gpsimd(r - 1)
-        back(15)
-        rope(15, 0)
-        add_vector(14)
-        store(14)
-        rope(15, 1)
-        adds_gpsimd(15)
-        add_vector(15)
-        store(15)
+        for r in range(1, LAST_DIRECT + 1):
+            mx(r)
+            w_in(r + 1, 0, "IN0")
+            w_in(r + 1, 1, "IN1")
+            back(r)
+            rope(r)
+            add_store(r)
+            w_quant(r + 1)
+        mx(LAST_DIRECT + 1)
+        for r in range(LAST_DIRECT + 2, N_ROUNDS):
+            mx(r)
+            back(r - 1)
+            rope(r - 1)
+            add_store(r - 1)
+        back(N_ROUNDS - 1)
+        rope(N_ROUNDS - 1)
+        add_store(N_ROUNDS - 1)

@@ -32,9 +32,9 @@ def tile_l1regressionmoeactionhead_pa_kernel(tc, x, W_qa, b_qa, W_qt, b_qt, out_
     with ExitStack() as ctx:
         keep = ctx.enter_context(tc.tile_pool(name="keep", bufs=1))
         wgp = ctx.enter_context(tc.tile_pool(name="wgp", bufs=3))
-        qsp = ctx.enter_context(tc.tile_pool(name="qsp", bufs=3))
-        abp = ctx.enter_context(tc.tile_pool(name="abp", bufs=5))
-        obp = ctx.enter_context(tc.tile_pool(name="obp", bufs=4))
+        qsp = ctx.enter_context(tc.tile_pool(name="qsp", bufs=4))
+        abp = ctx.enter_context(tc.tile_pool(name="abp", bufs=6))
+        obp = ctx.enter_context(tc.tile_pool(name="obp", bufs=6))
         psum = ctx.enter_context(tc.psum_pool(name="psum", bufs=1))
         ctx.enter_context(tc.manual_schedule())
 
@@ -151,8 +151,9 @@ def tile_l1regressionmoeactionhead_pa_kernel(tc, x, W_qa, b_qa, W_qt, b_qt, out_
 
         def mx(i):
             k, n = rounds[i]
+            spare = i > LAST_DIRECT and i % 2 == 0
             for m in range(2):
-                acc[(i, m)] = bank("ACC%d" % m)
+                acc[(i, m)] = bank(("IN%d" if spare else "ACC%d") % m)
                 for g in range(2):
                     s0 = P * (2 * m + g)
                     nc.tensor.matmul_mx(out=acc[(i, m)][:],

@@ -22,7 +22,7 @@ C2 = TWO_PI - C1
 RATIO = 10000.0 ** (-1.0 / 64.0)
 N_ROUNDS = 16
 LAST_DIRECT = 6
-FIRST_VECTOR_ADD = 14
+FIRST_VECTOR_ADD = 12
 
 
 def tile_l1regressionmoeactionhead_pa_kernel(tc, x, W_qa, b_qa, W_qt, b_qt, out_0, out_1):
@@ -32,9 +32,9 @@ def tile_l1regressionmoeactionhead_pa_kernel(tc, x, W_qa, b_qa, W_qt, b_qt, out_
     with ExitStack() as ctx:
         keep = ctx.enter_context(tc.tile_pool(name="keep", bufs=1))
         wgp = ctx.enter_context(tc.tile_pool(name="wgp", bufs=3))
-        qsp = ctx.enter_context(tc.tile_pool(name="qsp", bufs=4))
-        abp = ctx.enter_context(tc.tile_pool(name="abp", bufs=6))
-        obp = ctx.enter_context(tc.tile_pool(name="obp", bufs=6))
+        qsp = ctx.enter_context(tc.tile_pool(name="qsp", bufs=3))
+        abp = ctx.enter_context(tc.tile_pool(name="abp", bufs=8))
+        obp = ctx.enter_context(tc.tile_pool(name="obp", bufs=4))
         psum = ctx.enter_context(tc.psum_pool(name="psum", bufs=1))
         ctx.enter_context(tc.manual_schedule())
 
@@ -259,7 +259,9 @@ def tile_l1regressionmoeactionhead_pa_kernel(tc, x, W_qa, b_qa, W_qt, b_qt, out_
             mx(r)
             back(r - 1)
             rope(r - 1)
-            add_store(r - 1)
+            if r - 1 < FIRST_VECTOR_ADD:
+                add_store(r - 1)
         back(N_ROUNDS - 1)
         rope(N_ROUNDS - 1)
-        add_store(N_ROUNDS - 1)
+        for r in range(FIRST_VECTOR_ADD, N_ROUNDS):
+            add_store(r)

@@ -16,252 +16,249 @@ ACT = mybir.ActivationFunctionType
 P = 128
 FLOPS = 2 * 1024 * 1024 * 2048
 
-TWO_PI = 2.0 * math.pi
-C1 = 6.283203125
-C2 = TWO_PI - C1
-RATIO = 10000.0 ** (-1.0 / 64.0)
+N_GROUPS = 8
 N_ROUNDS = 16
-LAST_DIRECT = 6
-FIRST_VECTOR_ADD = 12
+LAST_INPUT_ROUND = N_GROUPS - 2
+GPSIMD_ROUNDS = 12
+
+TWO_PI = 2.0 * math.pi
+TWO_PI_HIGH = 6.283203125
+TWO_PI_LOW = TWO_PI - TWO_PI_HIGH
+FREQ_RATIO = 10000.0 ** (-1.0 / 64.0)
 
 
 def tile_l1regressionmoeactionhead_pa_kernel(tc, x, W_qa, b_qa, W_qt, b_qt, out_0, out_1):
     nc = tc.nc
     weights = [W_qa, W_qt]
     outs = [out_0, out_1]
+    rounds = [(0, 0), (1, 0), (0, 1), (1, 1)] + [(k, n) for k in range(2, N_GROUPS) for n in range(2)]
+
     with ExitStack() as ctx:
         keep = ctx.enter_context(tc.tile_pool(name="keep", bufs=1))
-        wgp = ctx.enter_context(tc.tile_pool(name="wgp", bufs=3))
-        qsp = ctx.enter_context(tc.tile_pool(name="qsp", bufs=3))
-        abp = ctx.enter_context(tc.tile_pool(name="abp", bufs=8))
-        obp = ctx.enter_context(tc.tile_pool(name="obp", bufs=4))
+        regrouped = ctx.enter_context(tc.tile_pool(name="regrouped", bufs=3))
+        biased = ctx.enter_context(tc.tile_pool(name="biased", bufs=3))
+        products = ctx.enter_context(tc.tile_pool(name="products", bufs=8))
+        results = ctx.enter_context(tc.tile_pool(name="results", bufs=4))
         psum = ctx.enter_context(tc.psum_pool(name="psum", bufs=1))
         ctx.enter_context(tc.manual_schedule())
 
         def bank(tag):
-            return psum.tile([P, 512], F32, name="bk" + tag, tag=tag)
+            return psum.tile([P, 512], F32, name="bank" + tag, tag=tag)
 
-        ident = keep.tile([P, P], F32, name="ident")
-        x_sb = [[keep.tile([P, 1024], BF16, name="x%d%d" % (n, j)) for j in range(4)] for n in range(2)]
-        w_sb = [keep.tile([P, 2048], BF16, name="w%d" % k) for k in range(8)]
-        xg = [keep.tile([P, 4096], BF16, name="xg%d" % n, align_bytes=64) for n in range(2)]
-        xcodes = [keep.tile([P, 1024], U32, name="xc%d" % n, align_bytes=64) for n in range(2)]
-        xscales = [keep.tile([P, 1024], U8, name="xs%d" % n, align_bytes=64) for n in range(2)]
-        wcodes = [keep.tile([P, 512], U32, name="wc%d" % k, align_bytes=64) for k in range(8)]
-        wscales = [keep.tile([P, 512], U8, name="ws%d" % k, align_bytes=64) for k in range(8)]
-        dm0 = keep.tile([P, 1], F32, name="dm0")
-        dm1 = keep.tile([P, 1], F32, name="dm1")
-        bz = keep.tile([P, 256], BF16, name="bz")
-        bf = keep.tile([P, 2, P], F32, name="bf")
-        bias_sb = keep.tile([P, 2, 8], F32, name="bias_sb")
+        identity = keep.tile([P, P], F32, name="identity")
+        x_rows = [[keep.tile([P, 1024], BF16, name="x%d%d" % (n, j)) for j in range(4)] for n in range(2)]
+        w_rows = [keep.tile([P, 2048], BF16, name="w%d" % k) for k in range(N_GROUPS)]
+        x_grouped = [keep.tile([P, 4096], BF16, name="xg%d" % n, align_bytes=64) for n in range(2)]
+        x_codes = [keep.tile([P, 1024], U32, name="xc%d" % n, align_bytes=64) for n in range(2)]
+        x_scales = [keep.tile([P, 1024], U8, name="xs%d" % n, align_bytes=64) for n in range(2)]
+        w_codes = [keep.tile([P, 512], U32, name="wc%d" % k, align_bytes=64) for k in range(N_GROUPS)]
+        w_scales = [keep.tile([P, 512], U8, name="ws%d" % k, align_bytes=64) for k in range(N_GROUPS)]
+        zero = keep.tile([P, 1], F32, name="zero")
+        unused = keep.tile([P, 1], F32, name="unused")
+        bias_rows = keep.tile([P, 256], BF16, name="bias_rows")
+        bias_split = keep.tile([P, 2, P], F32, name="bias_split")
+        bias = keep.tile([P, 2, N_GROUPS], F32, name="bias")
         freq = keep.tile([P, 64], F32, name="freq")
-        t_i = keep.tile([P, 4], I32, name="t_i")
-        t_f = keep.tile([P, 4], F32, name="t_f")
-        ang = keep.tile([P, 4, 64], F32, name="ang")
-        k_i = keep.tile([P, 4, 64], I32, name="k_i")
-        k_f = keep.tile([P, 4, 64], F32, name="k_f")
-        r1 = keep.tile([P, 4, 64], F32, name="r1")
-        r2 = keep.tile([P, 4, 64], F32, name="r2")
-        gs = keep.tile([P, 4, 64], F32, name="gs")
-        gc = keep.tile([P, 4, 64], F32, name="gc")
-        rs = keep.tile([P, 4, 64], F32, name="rs")
-        rc = keep.tile([P, 4, 64], F32, name="rc")
-        cos_t = keep.tile([P, 2, 4, 2, 32], F32, name="cos_t")
-        sin_t = keep.tile([P, 2, 4, 2, 32], F32, name="sin_t")
+        token_int = keep.tile([P, 4], I32, name="token_int")
+        token = keep.tile([P, 4], F32, name="token")
+        angle = keep.tile([P, 4, 64], F32, name="angle")
+        turns_int = keep.tile([P, 4, 64], I32, name="turns_int")
+        turns = keep.tile([P, 4, 64], F32, name="turns")
+        reduced_high = keep.tile([P, 4, 64], F32, name="reduced_high")
+        reduced = keep.tile([P, 4, 64], F32, name="reduced")
+        wrap_sin = keep.tile([P, 4, 64], F32, name="wrap_sin")
+        wrap_cos = keep.tile([P, 4, 64], F32, name="wrap_cos")
+        sin_arg = keep.tile([P, 4, 64], F32, name="sin_arg")
+        cos_arg = keep.tile([P, 4, 64], F32, name="cos_arg")
+        cos_table = keep.tile([P, 2, 4, 2, 32], F32, name="cos_table")
+        sin_table = keep.tile([P, 2, 4, 2, 32], F32, name="sin_table")
 
-        make_identity(nc, ident[:])
-        nc.gpsimd.iota(t_i[:], pattern=[[1, 4]], base=0, channel_multiplier=4)
-        nc.vector.memset(dm0[:], 0.0)
-        nc.vector.memset(bz[:], 0.0)
+        make_identity(nc, identity[:])
+        nc.gpsimd.iota(token_int[:], pattern=[[1, 4]], base=0, channel_multiplier=4)
+        nc.vector.memset(zero[:], 0.0)
+        nc.vector.memset(bias_rows[:], 0.0)
         nc.vector.memset(freq[:, 0:1], 1.0)
 
-        nc.scalar.dma_start(out=bz[0:4, :], in_=b_qa.rearrange("(r c) -> r c", c=256))
-        nc.scalar.dma_start(out=bz[4:8, :], in_=b_qt.rearrange("(r c) -> r c", c=256))
+        nc.scalar.dma_start(out=bias_rows[0:4, :], in_=b_qa.rearrange("(r c) -> r c", c=256))
+        nc.scalar.dma_start(out=bias_rows[4:8, :], in_=b_qt.rearrange("(r c) -> r c", c=256))
 
-        def load_w(k):
+        def load_group(k):
             rows = weights[k // 4][256 * (k % 4):256 * (k % 4) + 256, :]
-            nc.sync.dma_start(out=w_sb[k][:], in_=rows.rearrange("(p m) k -> p (m k)", m=2))
+            nc.sync.dma_start(out=w_rows[k][:], in_=rows.rearrange("(p m) k -> p (m k)", m=2))
 
-        def load_x(n):
-            view = x[n].rearrange("(p j) k -> p j k", j=4)
+        def load_batch(n):
+            by_token = x[n].rearrange("(p j) k -> p j k", j=4)
             for j in range(4):
-                nc.sync.dma_start(out=x_sb[n][j][:], in_=view[:, j, :])
+                nc.sync.dma_start(out=x_rows[n][j][:], in_=by_token[:, j, :])
 
-        load_w(0)
-        load_x(0)
-        load_w(1)
-        load_x(1)
-        for k in range(2, 8):
-            load_w(k)
+        load_group(0)
+        load_batch(0)
+        load_group(1)
+        load_batch(1)
+        for k in range(2, N_GROUPS):
+            load_group(k)
 
-        nc.scalar.activation(out=dm1[:], in_=dm0[:], func=ACT.Sin)
+        nc.scalar.activation(out=unused[:], in_=zero[:], func=ACT.Sin)
 
-        for c in range(1, 4):
-            nc.vector.tensor_scalar(out=freq[:, c:c + 1], in0=freq[:, 0:1], scalar1=RATIO ** c,
-                                    scalar2=None, op0=ALU.mult)
-        for a in range(1, 4):
-            nc.vector.tensor_scalar(out=freq[:, 4 * a:4 * a + 4], in0=freq[:, 0:4], scalar1=RATIO ** (4 * a),
-                                    scalar2=None, op0=ALU.mult)
-        for a in range(1, 4):
-            nc.vector.tensor_scalar(out=freq[:, 16 * a:16 * a + 16], in0=freq[:, 0:16], scalar1=RATIO ** (16 * a),
-                                    scalar2=None, op0=ALU.mult)
-        nc.vector.tensor_copy(out=t_f[:], in_=t_i[:])
-        nc.vector.tensor_tensor(out=ang[:], in0=freq[:].unsqueeze(1).to_broadcast([P, 4, 64]),
-                                in1=t_f[:].unsqueeze(2).to_broadcast([P, 4, 64]), op=ALU.mult)
-        nc.vector.tensor_scalar(out=k_i[:], in0=ang[:], scalar1=1.0 / TWO_PI, scalar2=None, op0=ALU.mult)
-        nc.vector.tensor_copy(out=k_f[:], in_=k_i[:])
-        nc.vector.tensor_copy(out=bf[:], in_=bz[:].rearrange("r (p m) -> r m p", m=2))
-        nc.vector.scalar_tensor_tensor(out=r1[:], in0=k_f[:], scalar=-C1, in1=ang[:], op0=ALU.mult, op1=ALU.add)
-        nc.vector.scalar_tensor_tensor(out=r2[:], in0=k_f[:], scalar=-C2, in1=r1[:], op0=ALU.mult, op1=ALU.add)
+        for width in (1, 4, 16):
+            for a in range(1, 4):
+                nc.vector.tensor_scalar(out=freq[:, width * a:width * (a + 1)], in0=freq[:, 0:width],
+                                        scalar1=FREQ_RATIO ** (width * a), scalar2=None, op0=ALU.mult)
+        nc.vector.tensor_copy(out=token[:], in_=token_int[:])
+        nc.vector.tensor_tensor(out=angle[:], in0=freq[:].unsqueeze(1).to_broadcast([P, 4, 64]),
+                                in1=token[:].unsqueeze(2).to_broadcast([P, 4, 64]), op=ALU.mult)
+        nc.vector.tensor_scalar(out=turns_int[:], in0=angle[:], scalar1=1.0 / TWO_PI, scalar2=None, op0=ALU.mult)
+        nc.vector.tensor_copy(out=turns[:], in_=turns_int[:])
+        nc.vector.tensor_copy(out=bias_split[:], in_=bias_rows[:].rearrange("r (p m) -> r m p", m=2))
+        nc.vector.scalar_tensor_tensor(out=reduced_high[:], in0=turns[:], scalar=-TWO_PI_HIGH, in1=angle[:],
+                                       op0=ALU.mult, op1=ALU.add)
+        nc.vector.scalar_tensor_tensor(out=reduced[:], in0=turns[:], scalar=-TWO_PI_LOW, in1=reduced_high[:],
+                                       op0=ALU.mult, op1=ALU.add)
 
-        def words_in(src32, tag):
-            bk = bank(tag)
+        def transpose_words(words, tag):
+            block = bank(tag)
             for q in range(4):
-                nc.tensor.transpose(bk[:, P * q:P * (q + 1)], src32[:, P * q:P * (q + 1)], ident[:])
-            return bk[:].rearrange("p (g u r) -> p g r u", g=2, u=2)
+                nc.tensor.transpose(block[:, P * q:P * (q + 1)], words[:, P * q:P * (q + 1)], identity[:])
+            return block[:].rearrange("p (g u r) -> p g r u", g=2, u=2)
 
-        wg = {}
+        w_grouped = {}
 
-        def w_in(k, m, tag):
+        def group_in(k, m, tag):
             if m == 0:
-                wg[k] = wgp.tile([P, 2048], BF16, name="wg", align_bytes=64)
-            src = words_in(w_sb[k][:].bitcast(F32)[:, 512 * m:512 * (m + 1)], tag)
-            dst = wg[k][:].bitcast(F32)[:, 512 * m:512 * (m + 1)].rearrange("p (g r u) -> p g r u", g=2, u=2)
-            nc.scalar.copy(out=dst, in_=src)
+                w_grouped[k] = regrouped.tile([P, 2048], BF16, name="wg", align_bytes=64)
+            blocks = transpose_words(w_rows[k][:].bitcast(F32)[:, 512 * m:512 * (m + 1)], tag)
+            words = w_grouped[k][:].bitcast(F32)[:, 512 * m:512 * (m + 1)]
+            nc.scalar.copy(out=words.rearrange("p (g r u) -> p g r u", g=2, u=2), in_=blocks)
 
-        def w_quant(k):
-            nc.vector.quantize_mx(out=wcodes[k][:].bitcast(FP8X4), scales=wscales[k][:], in_=wg[k][:])
+        def quantise_group(k):
+            nc.vector.quantize_mx(out=w_codes[k][:].bitcast(FP8X4), scales=w_scales[k][:], in_=w_grouped[k][:])
 
-        def x_in(n, j, tag):
-            src = words_in(x_sb[n][j][:].bitcast(F32), tag)
-            dst = xg[n][:].bitcast(F32).rearrange("p (g c u) -> p g c u", g=2, u=2)[:, :, P * j:P * (j + 1), :]
-            nc.scalar.copy(out=dst, in_=src)
+        def batch_in(n, j, tag):
+            blocks = transpose_words(x_rows[n][j][:].bitcast(F32), tag)
+            words = x_grouped[n][:].bitcast(F32).rearrange("p (g c u) -> p g c u", g=2, u=2)
+            nc.scalar.copy(out=words[:, :, P * j:P * (j + 1), :], in_=blocks)
 
-        def x_quant(n, j):
+        def quantise_batch(n, j):
             for g in range(2):
                 c0 = 512 * g + P * j
-                nc.vector.quantize_mx(out=xcodes[n][:, c0:c0 + P].bitcast(FP8X4), scales=xscales[n][:, c0:c0 + P],
-                                      in_=xg[n][:, 4 * c0:4 * (c0 + P)])
+                nc.vector.quantize_mx(out=x_codes[n][:, c0:c0 + P].bitcast(FP8X4), scales=x_scales[n][:, c0:c0 + P],
+                                      in_=x_grouped[n][:, 4 * c0:4 * (c0 + P)])
 
-        rounds = [(0, 0), (1, 0), (0, 1), (1, 1)] + [(k, n) for k in range(2, 8) for n in range(2)]
-        acc = {}
-        qs = {}
-        tb = {}
-        ab = {}
+        q_biased = {}
+        q_tokens = {}
+        halves = {}
 
-        def mx(i):
-            k, n = rounds[i]
-            spare = i > LAST_DIRECT and i % 2 == 0
+        def project(r):
+            k, n = rounds[r]
+            second_pair = r > LAST_INPUT_ROUND and r % 2 == 0
+            sums = {}
             for m in range(2):
-                acc[(i, m)] = bank(("IN%d" if spare else "ACC%d") % m)
+                sums[m] = bank(("IN%d" if second_pair else "ACC%d") % m)
                 for g in range(2):
                     s0 = P * (2 * m + g)
-                    nc.tensor.matmul_mx(out=acc[(i, m)][:],
-                                        lhsT=wcodes[k][:, s0:s0 + P].bitcast(FP8X4),
-                                        lhsT_scale=wscales[k][:, s0:s0 + P],
-                                        rhs=xcodes[n][:, 512 * g:512 * (g + 1)].bitcast(FP8X4),
-                                        rhs_scale=xscales[n][:, 512 * g:512 * (g + 1)],
+                    nc.tensor.matmul_mx(out=sums[m][:],
+                                        lhsT=w_codes[k][:, s0:s0 + P].bitcast(FP8X4),
+                                        lhsT_scale=w_scales[k][:, s0:s0 + P],
+                                        rhs=x_codes[n][:, 512 * g:512 * (g + 1)].bitcast(FP8X4),
+                                        rhs_scale=x_scales[n][:, 512 * g:512 * (g + 1)],
                                         start=(g == 0), stop=(g == 1))
             for m in range(2):
-                qs[(i, m)] = qsp.tile([P, 512], F32, name="qs%d" % m)
-                nc.scalar.activation(out=qs[(i, m)][:], in_=acc[(i, m)][:], func=ACT.Identity,
-                                     bias=bias_sb[:, m, k:k + 1], scale=1.0)
+                q_biased[(r, m)] = biased.tile([P, 512], F32, name="qb%d" % m)
+                nc.scalar.activation(out=q_biased[(r, m)][:], in_=sums[m][:], func=ACT.Identity,
+                                     bias=bias[:, m, k:k + 1], scale=1.0)
 
-        ident_hc = ident[:].rearrange("p (h c) -> p h c", h=2)
+        identity_by_head = identity[:].rearrange("p (h c) -> p h c", h=2)
 
-        def back(i):
+        def transpose_back(r):
             for m in range(2):
-                tb[(i, m)] = bank("T%d%d" % (i % 2, m))
-                by_head = tb[(i, m)][:].rearrange("p (h j c) -> p h j c", h=2, j=4)
+                q_tokens[(r, m)] = bank("T%d%d" % (r % 2, m))
+                by_head = q_tokens[(r, m)][:].rearrange("p (h j c) -> p h j c", h=2, j=4)
                 for j in range(4):
-                    nc.tensor.transpose(by_head[:, :, j, :], qs[(i, m)][:, P * j:P * (j + 1)], ident_hc)
+                    nc.tensor.transpose(by_head[:, :, j, :], q_biased[(r, m)][:, P * j:P * (j + 1)], identity_by_head)
 
-        def rope(i, tiles=(0, 1)):
-            if 0 in tiles:
-                ab[i] = abp.tile([P, 2, 2, 512], F32, name="ab")
-            for m in tiles:
-                tv = tb[(i, m)][:].rearrange("p (h c) -> p h c", h=2)
-                cos_v = cos_t[:, m].rearrange("p j r c -> p (j r c)").unsqueeze(1).to_broadcast([P, 2, 256])
-                sin_v = sin_t[:, 1 - m].rearrange("p j r c -> p (j r c)").unsqueeze(1).to_broadcast([P, 2, 256])
-                nc.vector.tensor_tensor(out=ab[i][:, 0, m, :].rearrange("p (h c) -> p h c", h=2), in0=tv,
-                                        in1=cos_v, op=ALU.mult)
-                nc.vector.tensor_tensor(out=ab[i][:, 1, 1 - m, :].rearrange("p (h c) -> p h c", h=2), in0=tv,
-                                        in1=sin_v, op=ALU.mult)
+        def multiply(r):
+            halves[r] = products.tile([P, 2, 2, 512], F32, name="halves")
+            for m in range(2):
+                q_v = q_tokens[(r, m)][:].rearrange("p (h c) -> p h c", h=2)
+                for which, table, e in ((0, cos_table, m), (1, sin_table, 1 - m)):
+                    both_heads = table[:, e].rearrange("p j r c -> p (j r c)").unsqueeze(1).to_broadcast([P, 2, 256])
+                    nc.vector.tensor_tensor(out=halves[r][:, which, e, :].rearrange("p (h c) -> p h c", h=2),
+                                            in0=q_v, in1=both_heads, op=ALU.mult)
 
-        def add_store(i):
-            k, n = rounds[i]
+        def add_and_store(r):
+            k, n = rounds[r]
             head = 2 * (k % 4)
-            dst = outs[k // 4][n, head:head + 2].rearrange("h (p j) d -> p h (j d)", j=4)
-            ob = obp.tile([P, 2, 512], F32, name="ob")
-            a_v = ab[i][:, 0].rearrange("p e c -> p c e")
-            b_v = ab[i][:, 1].rearrange("p e c -> p c e")
-            o_v = ob[:].rearrange("p h (c e) -> p (h c) e", e=2)
-            if i < FIRST_VECTOR_ADD:
-                nc.gpsimd.tensor_tensor(out=o_v, in0=a_v, in1=b_v, op=ALU.add)
-                nc.sync.dma_start(out=dst, in_=ob[:])
+            target = outs[k // 4][n, head:head + 2].rearrange("h (p j) d -> p h (j d)", j=4)
+            result = results.tile([P, 2, 512], F32, name="result")
+            cos_part = halves[r][:, 0].rearrange("p e c -> p c e")
+            sin_part = halves[r][:, 1].rearrange("p e c -> p c e")
+            total = result[:].rearrange("p h (c e) -> p (h c) e", e=2)
+            if r < GPSIMD_ROUNDS:
+                nc.gpsimd.tensor_tensor(out=total, in0=cos_part, in1=sin_part, op=ALU.add)
+                nc.sync.dma_start(out=target, in_=result[:])
             else:
                 for h in range(2):
                     cols = slice(256 * h, 256 * (h + 1))
-                    nc.vector.tensor_tensor(out=o_v[:, cols, :], in0=a_v[:, cols, :], in1=b_v[:, cols, :], op=ALU.add)
-                    nc.sync.dma_start(out=dst[:, h, :], in_=ob[:, h, :])
+                    nc.vector.tensor_tensor(out=total[:, cols, :], in0=cos_part[:, cols, :], in1=sin_part[:, cols, :],
+                                            op=ALU.add)
+                    nc.sync.dma_start(out=target[:, h, :], in_=result[:, h, :])
 
-        w_in(0, 0, "IN0")
-        w_in(0, 1, "IN1")
+        group_in(0, 0, "IN0")
+        group_in(0, 1, "IN1")
         for j in range(4):
-            x_in(0, j, "T%d%d" % (j // 2, j % 2))
+            batch_in(0, j, "T%d%d" % (j // 2, j % 2))
             if j == 0:
-                w_quant(0)
+                quantise_group(0)
             else:
-                x_quant(0, j - 1)
-        x_quant(0, 3)
-        nc.vector.tensor_scalar(out=gs[:], in0=r2[:], scalar1=math.pi, scalar2=-TWO_PI, op0=ALU.is_gt, op1=ALU.mult)
-        nc.vector.tensor_scalar(out=gc[:], in0=r2[:], scalar1=0.5 * math.pi, scalar2=-TWO_PI,
+                quantise_batch(0, j - 1)
+        quantise_batch(0, 3)
+        nc.vector.tensor_scalar(out=wrap_sin[:], in0=reduced[:], scalar1=math.pi, scalar2=-TWO_PI,
                                 op0=ALU.is_gt, op1=ALU.mult)
-        nc.vector.tensor_tensor(out=rs[:], in0=r2[:], in1=gs[:], op=ALU.add)
-        nc.vector.scalar_tensor_tensor(out=rc[:], in0=r2[:], scalar=0.5 * math.pi, in1=gc[:],
+        nc.vector.tensor_scalar(out=wrap_cos[:], in0=reduced[:], scalar1=0.5 * math.pi, scalar2=-TWO_PI,
+                                op0=ALU.is_gt, op1=ALU.mult)
+        nc.vector.tensor_tensor(out=sin_arg[:], in0=reduced[:], in1=wrap_sin[:], op=ALU.add)
+        nc.vector.scalar_tensor_tensor(out=cos_arg[:], in0=reduced[:], scalar=0.5 * math.pi, in1=wrap_cos[:],
                                        op0=ALU.add, op1=ALU.add)
-        bias_ps = bank("ACC1")
+        bias_bank = bank("ACC1")
         for m in range(2):
-            nc.tensor.transpose(bias_ps[:, P * m:P * (m + 1)], bf[:, m, :], ident[:])
-        nc.scalar.copy(out=bias_sb[:], in_=bias_ps[:, 0:256].rearrange("p (m r) -> p m r", m=2)[:, :, 0:8])
-        w_in(1, 0, "IN0")
-        w_in(1, 1, "IN1")
-        w_quant(1)
-        for e in range(2):
-            rc_v = rc[:].rearrange("p j (c e) -> p e j c", e=2)[:, e].unsqueeze(2).to_broadcast([P, 4, 2, 32])
-            rs_v = rs[:].rearrange("p j (c e) -> p e j c", e=2)[:, e].unsqueeze(2).to_broadcast([P, 4, 2, 32])
-            nc.scalar.activation(out=cos_t[:, e], in_=rc_v, func=ACT.Sin)
-            nc.scalar.activation(out=sin_t[:, e], in_=rs_v, func=ACT.Sin, scale=(-1.0 if e == 0 else 1.0))
-        mx(0)
-        x_in(1, 0, "T10")
-        x_in(1, 1, "T11")
-        x_in(1, 2, "IN0")
-        x_in(1, 3, "IN1")
-        back(0)
-        x_quant(1, 0)
-        x_quant(1, 1)
-        rope(0, (0,))
-        x_quant(1, 2)
-        x_quant(1, 3)
-        rope(0, (1,))
-        add_store(0)
+            nc.tensor.transpose(bias_bank[:, P * m:P * (m + 1)], bias_split[:, m, :], identity[:])
+        nc.scalar.copy(out=bias[:], in_=bias_bank[:, 0:256].rearrange("p (m r) -> p m r", m=2)[:, :, 0:N_GROUPS])
+        group_in(1, 0, "IN0")
+        group_in(1, 1, "IN1")
+        quantise_group(1)
 
-        for r in range(1, LAST_DIRECT + 1):
-            mx(r)
-            w_in(r + 1, 0, "IN0")
-            w_in(r + 1, 1, "IN1")
-            back(r)
-            rope(r)
-            add_store(r)
-            w_quant(r + 1)
-        mx(LAST_DIRECT + 1)
-        for r in range(LAST_DIRECT + 2, N_ROUNDS):
-            mx(r)
-            back(r - 1)
-            rope(r - 1)
-            if r - 1 < FIRST_VECTOR_ADD:
-                add_store(r - 1)
-        back(N_ROUNDS - 1)
-        rope(N_ROUNDS - 1)
-        for r in range(FIRST_VECTOR_ADD, N_ROUNDS):
-            add_store(r)
+        project(0)
+        for table, argument, e, sign in ((cos_table, cos_arg, 0, 1.0), (sin_table, sin_arg, 1, 1.0),
+                                         (cos_table, cos_arg, 1, 1.0), (sin_table, sin_arg, 0, -1.0)):
+            of_parity = argument[:].rearrange("p j (c e) -> p e j c", e=2)[:, e]
+            nc.scalar.activation(out=table[:, e], in_=of_parity.unsqueeze(2).to_broadcast([P, 4, 2, 32]), func=ACT.Sin,
+                                 scale=sign)
+        batch_in(1, 0, "T10")
+        batch_in(1, 1, "T11")
+        transpose_back(0)
+        batch_in(1, 2, "IN0")
+        batch_in(1, 3, "IN1")
+        multiply(0)
+        add_and_store(0)
+        for j in range(4):
+            quantise_batch(1, j)
+
+        for r in range(1, LAST_INPUT_ROUND + 1):
+            project(r)
+            group_in(r + 1, 0, "IN0")
+            group_in(r + 1, 1, "IN1")
+            transpose_back(r)
+            multiply(r)
+            add_and_store(r)
+            quantise_group(r + 1)
+
+        project(LAST_INPUT_ROUND + 1)
+        for r in range(LAST_INPUT_ROUND + 1, N_ROUNDS):
+            if r + 1 < N_ROUNDS:
+                project(r + 1)
+            transpose_back(r)
+            multiply(r)
+            if r < GPSIMD_ROUNDS:
+                add_and_store(r)
+        for r in range(GPSIMD_ROUNDS, N_ROUNDS):
+            add_and_store(r)

import math
from contextlib import ExitStack

import concourse.mybir as mybir
from concourse.masks import make_identity

F32 = mybir.dt.float32
BF16 = mybir.dt.bfloat16
I32 = mybir.dt.int32
U32 = mybir.dt.uint32
U8 = mybir.dt.uint8
FP8X4 = mybir.dt.float8_e4m3fn_x4
ALU = mybir.AluOpType
ACT = mybir.ActivationFunctionType

P = 128
FLOPS = 2 * 1024 * 1024 * 2048

N_GROUPS = 8
N_ROUNDS = 16
LAST_INPUT_ROUND = N_GROUPS - 2
GPSIMD_ROUNDS = 12

TWO_PI = 2.0 * math.pi
TWO_PI_HIGH = 6.283203125
TWO_PI_LOW = TWO_PI - TWO_PI_HIGH
FREQ_RATIO = 10000.0 ** (-1.0 / 64.0)


def tile_l1regressionmoeactionhead_pa_kernel(tc, x, W_qa, b_qa, W_qt, b_qt, out_0, out_1):
    nc = tc.nc
    weights = [W_qa, W_qt]
    outs = [out_0, out_1]
    rounds = [(0, 0), (1, 0), (0, 1), (1, 1)] + [(k, n) for k in range(2, N_GROUPS) for n in range(2)]

    with ExitStack() as ctx:
        keep = ctx.enter_context(tc.tile_pool(name="keep", bufs=1))
        regrouped = ctx.enter_context(tc.tile_pool(name="regrouped", bufs=3))
        biased = ctx.enter_context(tc.tile_pool(name="biased", bufs=3))
        products = ctx.enter_context(tc.tile_pool(name="products", bufs=8))
        results = ctx.enter_context(tc.tile_pool(name="results", bufs=4))
        psum = ctx.enter_context(tc.psum_pool(name="psum", bufs=1))
        ctx.enter_context(tc.manual_schedule())

        def bank(tag):
            return psum.tile([P, 512], F32, name="bank" + tag, tag=tag)

        identity = keep.tile([P, P], F32, name="identity")
        x_rows = [[keep.tile([P, 1024], BF16, name="x%d%d" % (n, j)) for j in range(4)] for n in range(2)]
        w_rows = [keep.tile([P, 2048], BF16, name="w%d" % k) for k in range(N_GROUPS)]
        x_grouped = [keep.tile([P, 4096], BF16, name="xg%d" % n, align_bytes=64) for n in range(2)]
        x_codes = [keep.tile([P, 1024], U32, name="xc%d" % n, align_bytes=64) for n in range(2)]
        x_scales = [keep.tile([P, 1024], U8, name="xs%d" % n, align_bytes=64) for n in range(2)]
        w_codes = [keep.tile([P, 512], U32, name="wc%d" % k, align_bytes=64) for k in range(N_GROUPS)]
        w_scales = [keep.tile([P, 512], U8, name="ws%d" % k, align_bytes=64) for k in range(N_GROUPS)]
        zero = keep.tile([P, 1], F32, name="zero")
        unused = keep.tile([P, 1], F32, name="unused")
        bias_rows = keep.tile([P, 256], BF16, name="bias_rows")
        bias_split = keep.tile([P, 2, P], F32, name="bias_split")
        bias = keep.tile([P, 2, N_GROUPS], F32, name="bias")
        freq = keep.tile([P, 64], F32, name="freq")
        token_int = keep.tile([P, 4], I32, name="token_int")
        token = keep.tile([P, 4], F32, name="token")
        angle = keep.tile([P, 4, 64], F32, name="angle")
        turns_int = keep.tile([P, 4, 64], I32, name="turns_int")
        turns = keep.tile([P, 4, 64], F32, name="turns")
        reduced_high = keep.tile([P, 4, 64], F32, name="reduced_high")
        reduced = keep.tile([P, 4, 64], F32, name="reduced")
        wrap_sin = keep.tile([P, 4, 64], F32, name="wrap_sin")
        wrap_cos = keep.tile([P, 4, 64], F32, name="wrap_cos")
        sin_arg = keep.tile([P, 4, 64], F32, name="sin_arg")
        cos_arg = keep.tile([P, 4, 64], F32, name="cos_arg")
        cos_table = keep.tile([P, 2, 4, 2, 32], F32, name="cos_table")
        sin_table = keep.tile([P, 2, 4, 2, 32], F32, name="sin_table")

        make_identity(nc, identity[:])
        nc.gpsimd.iota(token_int[:], pattern=[[1, 4]], base=0, channel_multiplier=4)
        nc.vector.memset(zero[:], 0.0)
        nc.vector.memset(bias_rows[:], 0.0)
        nc.vector.memset(freq[:, 0:1], 1.0)

        nc.scalar.dma_start(out=bias_rows[0:4, :], in_=b_qa.rearrange("(r c) -> r c", c=256))
        nc.scalar.dma_start(out=bias_rows[4:8, :], in_=b_qt.rearrange("(r c) -> r c", c=256))

        def load_group(k):
            rows = weights[k // 4][256 * (k % 4):256 * (k % 4) + 256, :]
            nc.sync.dma_start(out=w_rows[k][:], in_=rows.rearrange("(p m) k -> p (m k)", m=2))

        def load_batch(n):
            by_token = x[n].rearrange("(p j) k -> p j k", j=4)
            for j in range(4):
                nc.sync.dma_start(out=x_rows[n][j][:], in_=by_token[:, j, :])

        load_group(0)
        load_batch(0)
        load_group(1)
        load_batch(1)
        for k in range(2, N_GROUPS):
            load_group(k)

        nc.scalar.activation(out=unused[:], in_=zero[:], func=ACT.Sin)

        for width in (1, 4, 16):
            for a in range(1, 4):
                nc.vector.tensor_scalar(out=freq[:, width * a:width * (a + 1)], in0=freq[:, 0:width],
                                        scalar1=FREQ_RATIO ** (width * a), scalar2=None, op0=ALU.mult)
        nc.vector.tensor_copy(out=token[:], in_=token_int[:])
        nc.vector.tensor_tensor(out=angle[:], in0=freq[:].unsqueeze(1).to_broadcast([P, 4, 64]),
                                in1=token[:].unsqueeze(2).to_broadcast([P, 4, 64]), op=ALU.mult)
        nc.vector.tensor_scalar(out=turns_int[:], in0=angle[:], scalar1=1.0 / TWO_PI, scalar2=None, op0=ALU.mult)
        nc.vector.tensor_copy(out=turns[:], in_=turns_int[:])
        nc.vector.tensor_copy(out=bias_split[:], in_=bias_rows[:].rearrange("r (p m) -> r m p", m=2))
        nc.vector.scalar_tensor_tensor(out=reduced_high[:], in0=turns[:], scalar=-TWO_PI_HIGH, in1=angle[:],
                                       op0=ALU.mult, op1=ALU.add)
        nc.vector.scalar_tensor_tensor(out=reduced[:], in0=turns[:], scalar=-TWO_PI_LOW, in1=reduced_high[:],
                                       op0=ALU.mult, op1=ALU.add)

        def transpose_words(words, tag):
            block = bank(tag)
            for q in range(4):
                nc.tensor.transpose(block[:, P * q:P * (q + 1)], words[:, P * q:P * (q + 1)], identity[:])
            return block[:].rearrange("p (g u r) -> p g r u", g=2, u=2)

        w_grouped = {}

        def group_in(k, m, tag):
            if m == 0:
                w_grouped[k] = regrouped.tile([P, 2048], BF16, name="wg", align_bytes=64)
            blocks = transpose_words(w_rows[k][:].bitcast(F32)[:, 512 * m:512 * (m + 1)], tag)
            words = w_grouped[k][:].bitcast(F32)[:, 512 * m:512 * (m + 1)]
            nc.scalar.copy(out=words.rearrange("p (g r u) -> p g r u", g=2, u=2), in_=blocks)

        def quantise_group(k):
            nc.vector.quantize_mx(out=w_codes[k][:].bitcast(FP8X4), scales=w_scales[k][:], in_=w_grouped[k][:])

        def batch_in(n, j, tag):
            blocks = transpose_words(x_rows[n][j][:].bitcast(F32), tag)
            words = x_grouped[n][:].bitcast(F32).rearrange("p (g c u) -> p g c u", g=2, u=2)
            nc.scalar.copy(out=words[:, :, P * j:P * (j + 1), :], in_=blocks)

        def quantise_batch(n, j):
            for g in range(2):
                c0 = 512 * g + P * j
                nc.vector.quantize_mx(out=x_codes[n][:, c0:c0 + P].bitcast(FP8X4), scales=x_scales[n][:, c0:c0 + P],
                                      in_=x_grouped[n][:, 4 * c0:4 * (c0 + P)])

        q_biased = {}
        q_tokens = {}
        halves = {}

        def project(r):
            k, n = rounds[r]
            second_pair = r > LAST_INPUT_ROUND and r % 2 == 0
            sums = {}
            for m in range(2):
                sums[m] = bank(("IN%d" if second_pair else "ACC%d") % m)
                for g in range(2):
                    s0 = P * (2 * m + g)
                    nc.tensor.matmul_mx(out=sums[m][:],
                                        lhsT=w_codes[k][:, s0:s0 + P].bitcast(FP8X4),
                                        lhsT_scale=w_scales[k][:, s0:s0 + P],
                                        rhs=x_codes[n][:, 512 * g:512 * (g + 1)].bitcast(FP8X4),
                                        rhs_scale=x_scales[n][:, 512 * g:512 * (g + 1)],
                                        start=(g == 0), stop=(g == 1))
            for m in range(2):
                q_biased[(r, m)] = biased.tile([P, 512], F32, name="qb%d" % m)
                nc.scalar.activation(out=q_biased[(r, m)][:], in_=sums[m][:], func=ACT.Identity,
                                     bias=bias[:, m, k:k + 1], scale=1.0)

        identity_by_head = identity[:].rearrange("p (h c) -> p h c", h=2)

        def transpose_back(r):
            for m in range(2):
                q_tokens[(r, m)] = bank("T%d%d" % (r % 2, m))
                by_head = q_tokens[(r, m)][:].rearrange("p (h j c) -> p h j c", h=2, j=4)
                for j in range(4):
                    nc.tensor.transpose(by_head[:, :, j, :], q_biased[(r, m)][:, P * j:P * (j + 1)], identity_by_head)

        def multiply(r):
            halves[r] = products.tile([P, 2, 2, 512], F32, name="halves")
            for m in range(2):
                q_v = q_tokens[(r, m)][:].rearrange("p (h c) -> p h c", h=2)
                for which, table, e in ((0, cos_table, m), (1, sin_table, 1 - m)):
                    both_heads = table[:, e].rearrange("p j r c -> p (j r c)").unsqueeze(1).to_broadcast([P, 2, 256])
                    nc.vector.tensor_tensor(out=halves[r][:, which, e, :].rearrange("p (h c) -> p h c", h=2),
                                            in0=q_v, in1=both_heads, op=ALU.mult)

        def add_and_store(r):
            k, n = rounds[r]
            head = 2 * (k % 4)
            target = outs[k // 4][n, head:head + 2].rearrange("h (p j) d -> p h (j d)", j=4)
            result = results.tile([P, 2, 512], F32, name="result")
            cos_part = halves[r][:, 0].rearrange("p e c -> p c e")
            sin_part = halves[r][:, 1].rearrange("p e c -> p c e")
            total = result[:].rearrange("p h (c e) -> p (h c) e", e=2)
            if r < GPSIMD_ROUNDS:
                nc.gpsimd.tensor_tensor(out=total, in0=cos_part, in1=sin_part, op=ALU.add)
                nc.sync.dma_start(out=target, in_=result[:])
            else:
                for h in range(2):
                    cols = slice(256 * h, 256 * (h + 1))
                    nc.vector.tensor_tensor(out=total[:, cols, :], in0=cos_part[:, cols, :], in1=sin_part[:, cols, :],
                                            op=ALU.add)
                    nc.sync.dma_start(out=target[:, h, :], in_=result[:, h, :])

        group_in(0, 0, "IN0")
        group_in(0, 1, "IN1")
        for j in range(4):
            batch_in(0, j, "T%d%d" % (j // 2, j % 2))
            if j == 0:
                quantise_group(0)
            else:
                quantise_batch(0, j - 1)
        quantise_batch(0, 3)
        nc.vector.tensor_scalar(out=wrap_sin[:], in0=reduced[:], scalar1=math.pi, scalar2=-TWO_PI,
                                op0=ALU.is_gt, op1=ALU.mult)
        nc.vector.tensor_scalar(out=wrap_cos[:], in0=reduced[:], scalar1=0.5 * math.pi, scalar2=-TWO_PI,
                                op0=ALU.is_gt, op1=ALU.mult)
        nc.vector.tensor_tensor(out=sin_arg[:], in0=reduced[:], in1=wrap_sin[:], op=ALU.add)
        nc.vector.scalar_tensor_tensor(out=cos_arg[:], in0=reduced[:], scalar=0.5 * math.pi, in1=wrap_cos[:],
                                       op0=ALU.add, op1=ALU.add)
        bias_bank = bank("ACC1")
        for m in range(2):
            nc.tensor.transpose(bias_bank[:, P * m:P * (m + 1)], bias_split[:, m, :], identity[:])
        nc.scalar.copy(out=bias[:], in_=bias_bank[:, 0:256].rearrange("p (m r) -> p m r", m=2)[:, :, 0:N_GROUPS])
        group_in(1, 0, "IN0")
        group_in(1, 1, "IN1")
        quantise_group(1)

        project(0)
        for table, argument, e, sign in ((cos_table, cos_arg, 0, 1.0), (sin_table, sin_arg, 1, 1.0),
                                         (cos_table, cos_arg, 1, 1.0), (sin_table, sin_arg, 0, -1.0)):
            of_parity = argument[:].rearrange("p j (c e) -> p e j c", e=2)[:, e]
            nc.scalar.activation(out=table[:, e], in_=of_parity.unsqueeze(2).to_broadcast([P, 4, 2, 32]), func=ACT.Sin,
                                 scale=sign)
        batch_in(1, 0, "T10")
        batch_in(1, 1, "T11")
        transpose_back(0)
        batch_in(1, 2, "IN0")
        batch_in(1, 3, "IN1")
        multiply(0)
        add_and_store(0)
        for j in range(4):
            quantise_batch(1, j)

        for r in range(1, LAST_INPUT_ROUND + 1):
            project(r)
            group_in(r + 1, 0, "IN0")
            group_in(r + 1, 1, "IN1")
            transpose_back(r)
            multiply(r)
            add_and_store(r)
            quantise_group(r + 1)

        project(LAST_INPUT_ROUND + 1)
        for r in range(LAST_INPUT_ROUND + 1, N_ROUNDS):
            if r + 1 < N_ROUNDS:
                project(r + 1)
            transpose_back(r)
            multiply(r)
            if r < GPSIMD_ROUNDS:
                add_and_store(r)
        for r in range(GPSIMD_ROUNDS, N_ROUNDS):
            add_and_store(r)
